import numpy as np
import ml_dtypes


def mxq(x, axis, fmt="e4m3"):
    dtype, down = {"e4m3": (ml_dtypes.float8_e4m3fn, 7), "e5m2": (ml_dtypes.float8_e5m2, 14)}[fmt]
    v = np.moveaxis(np.asarray(x, np.float32).astype(ml_dtypes.bfloat16).astype(np.float64), axis, -1)
    blocks = v.reshape(v.shape[:-1] + (-1, 32))
    amax = np.abs(blocks).max(-1, keepdims=True)
    byte = np.maximum(np.where(amax > 0, np.frexp(amax)[1] - 1 + 127, 0) - down, 1)
    scale = np.exp2(byte - 127.0)
    codes = (blocks / scale).astype(np.float32).astype(dtype).astype(np.float64)
    return np.moveaxis((codes * scale).reshape(v.shape), -1, axis)


WIDE = False


def mx_kscale(k):
    if not WIDE:
        return np.ones(k)
    levels = np.array([10, -10, 5, -5, 0])
    if k % 512:
        return np.exp2(np.random.permutation(np.resize(levels, k // 32))).repeat(32)
    a = np.empty((k // 512, 16))
    for p in range(k // 512):
        a[p, :8] = np.random.permutation(np.resize(levels, 8))
        for g in range(8):
            far = levels[np.abs(levels - a[p, g]) >= 10]
            a[p, g + 8] = far[np.random.randint(len(far))]
    return np.exp2(a.ravel()).repeat(32)


BF16 = ml_dtypes.bfloat16


def bf(x):
    return np.asarray(x, np.float32).astype(BF16)


def f64(x):
    return np.asarray(x).astype(np.float64)


B, Nb1, Nw1, Nb2x, Nb2y, Nw2x, Nw2y, R, C = 128, 4, 16, 4, 2, 16, 16, 128, 2
J1 = Nb1 * Nb1
K1 = C * Nw1 * Nw1
J3 = Nb2x * Nb2y
L1 = J3 * R
J2 = J3 * J1


def setup_inputs():
    s = mx_kscale(K1)
    sx = s.reshape(Nw1, Nw1, C)[:, None, :, :]
    x = np.random.standard_normal((B, Nb1, Nw1, Nb1, Nw1, C)) * sx
    return {"x": bf(x.reshape(B, Nb1 * Nw1 * Nb1 * Nw1, C)),
            "k1": bf(np.random.standard_normal((J1, K1, L1)) / np.sqrt(K1) / s[None, :, None]),
            "b1": bf(np.random.standard_normal((1, J1, L1)) * 0.3)}


def core(x, k1, b1):
    h = f64(x).reshape(B, Nb1, Nw1, Nb1, Nw1, C).transpose(0, 1, 3, 2, 4, 5).reshape(B, J1, K1)
    hq = mxq(h, 2, "e4m3").transpose(1, 0, 2)
    y = (hq @ mxq(f64(k1), 1, "e4m3")).transpose(1, 0, 2) + f64(b1)
    y = y.reshape(B, J1, J3, R).transpose(0, 3, 1, 2)
    return y.reshape(B, J2, R)


def e4m3fn_bytes(y):
    return np.clip(np.asarray(y, np.float64), -448.0, 448.0).astype(np.float32).astype(ml_dtypes.float8_e4m3fn).view(np.uint8)


def reference(x, k1, b1):
    out = core(x, k1, b1)
    s = np.max(np.abs(out)) / 448.0
    return out, e4m3fn_bytes(out / s)

@@ -1,0 +1,226 @@
+from contextlib import ExitStack
+
+import concourse.mybir as mybir
+from concourse.masks import make_identity
+
+F32 = mybir.dt.float32
+BF16 = mybir.dt.bfloat16
+U32 = mybir.dt.uint32
+U8 = mybir.dt.uint8
+FP8X4 = mybir.dt.float8_e4m3fn_x4
+FP8 = mybir.dt.float8_e4m3fn
+ALU = mybir.AluOpType
+ACT = mybir.ActivationFunctionType
+AX = mybir.AxisListType
+
+P = 128
+NB = 128
+NJ = 16
+NK = 512
+NL = 1024
+NR = 128
+NM = 8
+HALF = 512
+FLOPS = 2 * NB * NJ * NK * NL
+
+CV = 352
+VS = 2688
+NRED = 8
+NST = 8
+NCAST = 4
+
+
+def tile_switchnet_fstar_pa_kernel(tc, x, k1, b1, out_0, out_1):
+    nc = tc.nc
+    x_v = x.rearrange("b (q g) c -> b q (g c)", q=4)
+    b_v = b1.rearrange("o j l -> (o j l)")
+    o0_v = out_0.rearrange("b r c -> b (r c)")
+    o1_v = out_1.rearrange("b r c -> b (r c)")
+
+    with ExitStack() as ctx:
+        const = ctx.enter_context(tc.tile_pool(name="const", bufs=1))
+        xpool = ctx.enter_context(tc.tile_pool(name="xpool", bufs=2))
+        kpool = ctx.enter_context(tc.tile_pool(name="kpool", bufs=3))
+        ps_x = ctx.enter_context(tc.psum_pool(name="ps_x", bufs=2))
+        ps_a = ctx.enter_context(tc.psum_pool(name="ps_a", bufs=4))
+        ps_t = ctx.enter_context(tc.psum_pool(name="ps_t", bufs=1))
+
+        zeros = const.tile([P, 1], F32, name="zeros")
+        warm = const.tile([P, 1], F32, name="warm")
+        ident = const.tile([P, P], F32, name="ident")
+        hcodes = const.tile([P, NJ * NB], U32, name="hcodes", align_bytes=64)
+        hscales = const.tile([P, NJ * NB], U8, name="hscales", align_bytes=64)
+        y = const.tile([P, NR, NJ * NM], F32, name="y")
+        stats = const.tile([P, NRED], F32, name="stats")
+        pmax = const.tile([P, 1], F32, name="pmax")
+        amax = const.tile([P, 1], F32, name="amax")
+        rcp = const.tile([P, 1], F32, name="rcp")
+        fac = const.tile([P, 1], F32, name="fac")
+        bias = []
+        for g in range(4):
+            bias_g = const.tile([P, 4 * NL], BF16, name="bias%d" % g)
+            bias.append(bias_g)
+
+        nc.vector.memset(zeros[:], 0.0)
+        nc.scalar.activation(out=warm[:], in_=zeros[:], func=ACT.Identity)
+        make_identity(nc, ident[:])
+
+        raws = {}
+        grps = {}
+        codes = {}
+        accs = {}
+
+        def load_k(j):
+            raw = kpool.tile([P, 4, NL], BF16, name="raw", bufs=4)
+            nc.sync.dma_start(out=raw[:], in_=k1[j].rearrange("(p t) c -> p t c", t=4))
+            raws[j] = raw
+
+        def load_bias(g):
+            nc.sync.dma_start(
+                out=bias[g][:], in_=b_v[g * 4 * NL : (g + 1) * 4 * NL].partition_broadcast(P)
+            )
+
+        def interleave(j):
+            raw = raws[j]
+            grp = kpool.tile([P, NL, 4], BF16, name="grp", align_bytes=64)
+            nc.vector.tensor_copy(
+                out=grp[:, 0:CV, :], in_=raw[:, :, 0:CV].rearrange("p t c -> p c t")
+            )
+            nc.scalar.copy(
+                out=grp[:, CV:NL, :], in_=raw[:, :, CV:NL].rearrange("p t c -> p c t")
+            )
+            grps[j] = grp
+
+        def quantize(j):
+            kc = kpool.tile([P, NL], U32, name="kc", align_bytes=64)
+            ks = kpool.tile([P, NL], U8, name="ks", align_bytes=64)
+            nc.vector.quantize_mx(
+                out=kc[:].bitcast(FP8X4),
+                scales=ks[:],
+                in_=grps[j][:].rearrange("p c t -> p (c t)"),
+            )
+            codes[j] = (kc, ks)
+
+        def matmul(j):
+            kc, ks = codes[j]
+            for hf in range(2):
+                acc = ps_a.tile([P, HALF], F32, name="acc")
+                nc.tensor.matmul_mx(
+                    out=acc[:],
+                    lhsT=hcodes[:, j * NB : (j + 1) * NB].bitcast(FP8X4),
+                    lhsT_scale=hscales[:, j * NB : (j + 1) * NB],
+                    rhs=kc[:, hf * HALF : (hf + 1) * HALF].bitcast(FP8X4),
+                    rhs_scale=ks[:, hf * HALF : (hf + 1) * HALF],
+                    start=True,
+                    stop=True,
+                )
+                accs[(j, hf)] = acc
+
+        def evacuate(j):
+            for hf in range(2):
+                c0 = j * NM + hf * 4
+                b0 = (j % 4) * NL + hf * HALF
+                nc.vector.tensor_tensor(
+                    out=y[:, :, c0 : c0 + 4],
+                    in0=accs[(j, hf)][:].rearrange("p (m r) -> p r m", m=4),
+                    in1=bias[j // 4][:, b0 : b0 + HALF].rearrange("p (m r) -> p r m", m=4),
+                    op=ALU.add,
+                )
+
+        load_k(0)
+        xs = []
+        for br in range(4):
+            xs_t = xpool.tile([P, 2048], BF16, name="xs", bufs=4)
+            nc.sync.dma_start(out=xs_t[:], in_=x_v[:, br, :])
+            xs.append(xs_t)
+        load_k(1)
+        load_k(2)
+        load_bias(0)
+        load_k(3)
+
+        interleave(0)
+
+        for br in range(4):
+            xh = xpool.tile([P, 2048], BF16, name="xh")
+            nc.vector.tensor_copy(
+                out=xh[:].rearrange("p (c r e) -> p c r e", c=4, r=16),
+                in_=xs[br][:].rearrange("p (r c e) -> p c r e", r=16, c=4),
+            )
+            words = xh[:].bitcast(F32)
+            hg = xpool.tile([P, 2048], BF16, name="hg", align_bytes=64)
+            hgw = hg[:].bitcast(F32)
+            for h2 in range(2):
+                xt = ps_x.tile([P, 512], F32, name="xt")
+                for jj in range(2):
+                    for u in range(2):
+                        w0 = (h2 * 2 + jj) * 256
+                        nc.tensor.transpose(
+                            xt[:, (jj * 2 + u) * P : (jj * 2 + u + 1) * P],
+                            words[:, w0 + u : w0 + 256 : 2],
+                            ident[:],
+                        )
+                nc.scalar.copy(
+                    out=hgw[:, h2 * 512 : (h2 + 1) * 512].rearrange(
+                        "p (j b u) -> p j b u", j=2, u=2
+                    ),
+                    in_=xt[:].rearrange("p (j u b) -> p j b u", j=2, u=2),
+                )
+            nc.vector.quantize_mx(
+                out=hcodes[:, br * 512 : (br + 1) * 512].bitcast(FP8X4),
+                scales=hscales[:, br * 512 : (br + 1) * 512],
+                in_=hg[:],
+            )
+
+        for j in range(NJ):
+            if j + 1 < NJ:
+                interleave(j + 1)
+            quantize(j)
+            if j + 4 < NJ:
+                load_k(j + 4)
+            if j % 4 == 1 and j // 4 + 1 < 4:
+                load_bias(j // 4 + 1)
+            if j >= 1:
+                evacuate(j - 1)
+            matmul(j)
+        evacuate(NJ - 1)
+
+        yf = y[:].rearrange("p r c -> p (r c)")
+        wst = NR * NJ * NM // NST
+        for s in range(NST):
+            nc.sync.dma_start(out=o0_v[:, s * wst : (s + 1) * wst], in_=yf[:, s * wst : (s + 1) * wst])
+        wred = NR * NJ * NM // NRED
+        for s in range(NRED):
+            nc.vector.tensor_reduce(
+                out=stats[:, s : s + 1],
+                in_=yf[:, s * wred : (s + 1) * wred],
+                axis=AX.X,
+                op=ALU.max,
+                apply_absolute_value=True,
+            )
+        nc.vector.tensor_reduce(out=pmax[:], in_=stats[:], axis=AX.X, op=ALU.max)
+        tp = ps_t.tile([P, P], F32, name="tp")
+        nc.tensor.transpose(tp[:], pmax[:, 0:1].to_broadcast([P, P]), ident[:])
+        nc.vector.tensor_reduce(out=amax[:], in_=tp[:], axis=AX.X, op=ALU.max)
+        nc.vector.reciprocal(out=rcp[:], in_=amax[:])
+        nc.vector.tensor_scalar(out=fac[:], in0=rcp[:], scalar1=448.0, scalar2=None, op0=ALU.mult)
+
+        wc = NR * NJ * NM // NCAST
+        for q in range(NCAST):
+            f8 = const.tile([P, wc], FP8, name="f8_%d" % q)
+            nc.vector.tensor_scalar(
+                out=f8[:, 0:VS],
+                in0=yf[:, q * wc : q * wc + VS],
+                scalar1=fac[:, 0:1],
+                scalar2=None,
+                op0=ALU.mult,
+                saturate=False,
+            )
+            nc.scalar.activation(
+                out=f8[:, VS:wc],
+                in_=yf[:, q * wc + VS : (q + 1) * wc],
+                func=ACT.Identity,
+                scale=fac[:, 0:1],
+                bias=zeros[:, 0:1],
+                saturate=False,
+            )
+            nc.sync.dma_start(out=o1_v[:, q * wc : (q + 1) * wc], in_=f8[:].bitcast(U8))

@@ -84,10 +84,12 @@ def tile_switchnet_fstar_pa_kernel(tc, x, k1, b1, out_0, out_1):
             raw = raws[j]
             grp = kpool.tile([P, NL, 4], BF16, name="grp", align_bytes=64)
             nc.vector.tensor_copy(
-                out=grp[:, 0:CV, :], in_=raw[:, :, 0:CV].rearrange("p t c -> p c t")
+                out=grp[:, 0:CV, :].rearrange("p (c i) t -> p c t i", i=4),
+                in_=raw[:, :, 0:CV].rearrange("p t (c i) -> p c t i", i=4),
             )
             nc.scalar.copy(
-                out=grp[:, CV:NL, :], in_=raw[:, :, CV:NL].rearrange("p t c -> p c t")
+                out=grp[:, CV:NL, :].rearrange("p (c i) t -> p c t i", i=4),
+                in_=raw[:, :, CV:NL].rearrange("p t (c i) -> p c t i", i=4),
             )
             grps[j] = grp
 

@@ -23,11 +23,11 @@ NM = 8
 HALF = 512
 FLOPS = 2 * NB * NJ * NK * NL
 
-CV = 352
-VS = 2688
+CV = 448
 NRED = 8
 NST = 8
-NCAST = 4
+CASTS = [(0, 4096), (4096, 4096), (8192, 4096), (12288, 2048), (14336, 2048)]
+VSHARE = 21
 
 
 def tile_switchnet_fstar_pa_kernel(tc, x, k1, b1, out_0, out_1):
@@ -39,7 +39,6 @@ def tile_switchnet_fstar_pa_kernel(tc, x, k1, b1, out_0, out_1):
 
     with ExitStack() as ctx:
         const = ctx.enter_context(tc.tile_pool(name="const", bufs=1))
-        xpool = ctx.enter_context(tc.tile_pool(name="xpool", bufs=2))
         kpool = ctx.enter_context(tc.tile_pool(name="kpool", bufs=3))
         ps_x = ctx.enter_context(tc.psum_pool(name="ps_x", bufs=2))
         ps_a = ctx.enter_context(tc.psum_pool(name="ps_a", bufs=4))
@@ -60,6 +59,7 @@ def tile_switchnet_fstar_pa_kernel(tc, x, k1, b1, out_0, out_1):
         for g in range(4):
             bias_g = const.tile([P, 4 * NL], BF16, name="bias%d" % g)
             bias.append(bias_g)
+        yf = y[:].rearrange("p r c -> p (r c)")
 
         nc.vector.memset(zeros[:], 0.0)
         nc.scalar.activation(out=warm[:], in_=zeros[:], func=ACT.Identity)
@@ -70,9 +70,14 @@ def tile_switchnet_fstar_pa_kernel(tc, x, k1, b1, out_0, out_1):
         codes = {}
         accs = {}
 
-        def load_k(j):
+        def split(j):
+            return HALF if j == NJ - 1 else CV
+
+        def load_k(j, cuts):
             raw = kpool.tile([P, 4, NL], BF16, name="raw", bufs=4)
-            nc.sync.dma_start(out=raw[:], in_=k1[j].rearrange("(p t) c -> p t c", t=4))
+            src = k1[j].rearrange("(p t) c -> p t c", t=4)
+            for a, b in cuts:
+                nc.sync.dma_start(out=raw[:, :, a:b], in_=src[:, :, a:b])
             raws[j] = raw
 
         def load_bias(g):
@@ -80,27 +85,28 @@ def tile_switchnet_fstar_pa_kernel(tc, x, k1, b1, out_0, out_1):
                 out=bias[g][:], in_=b_v[g * 4 * NL : (g + 1) * 4 * NL].partition_broadcast(P)
             )
 
+        def lace(eng_copy, grp, raw, a, b):
+            eng_copy(
+                out=grp[:, a:b, :].rearrange("p (c i) t -> p c t i", i=4),
+                in_=raw[:, :, a:b].rearrange("p t (c i) -> p c t i", i=4),
+            )
+
         def interleave(j):
-            raw = raws[j]
             grp = kpool.tile([P, NL, 4], BF16, name="grp", align_bytes=64)
-            nc.vector.tensor_copy(
-                out=grp[:, 0:CV, :].rearrange("p (c i) t -> p c t i", i=4),
-                in_=raw[:, :, 0:CV].rearrange("p t (c i) -> p c t i", i=4),
-            )
-            nc.scalar.copy(
-                out=grp[:, CV:NL, :].rearrange("p (c i) t -> p c t i", i=4),
-                in_=raw[:, :, CV:NL].rearrange("p t (c i) -> p c t i", i=4),
-            )
+            lace(nc.vector.tensor_copy, grp, raws[j], 0, split(j))
+            lace(nc.scalar.copy, grp, raws[j], split(j), NL)
             grps[j] = grp
 
         def quantize(j):
             kc = kpool.tile([P, NL], U32, name="kc", align_bytes=64)
             ks = kpool.tile([P, NL], U8, name="ks", align_bytes=64)
-            nc.vector.quantize_mx(
-                out=kc[:].bitcast(FP8X4),
-                scales=ks[:],
-                in_=grps[j][:].rearrange("p c t -> p (c t)"),
-            )
+            cuts = [(0, HALF), (HALF, NL)] if j == NJ - 1 else [(0, NL)]
+            for a, b in cuts:
+                nc.vector.quantize_mx(
+                    out=kc[:, a:b].bitcast(FP8X4),
+                    scales=ks[:, a:b],
+                    in_=grps[j][:, a:b, :].rearrange("p c t -> p (c t)"),
+                )
             codes[j] = (kc, ks)
 
         def matmul(j):
@@ -129,56 +135,62 @@ def tile_switchnet_fstar_pa_kernel(tc, x, k1, b1, out_0, out_1):
                     op=ALU.add,
                 )
 
-        load_k(0)
-        xs = []
-        for br in range(4):
-            xs_t = xpool.tile([P, 2048], BF16, name="xs", bufs=4)
-            nc.sync.dma_start(out=xs_t[:], in_=x_v[:, br, :])
-            xs.append(xs_t)
-        load_k(1)
-        load_k(2)
-        load_bias(0)
-        load_k(3)
+        load_k(0, [(CV, NL), (0, CV)])
+        with tc.tile_pool(name="xpool", bufs=2) as xpool:
+            xs = []
+            for br in range(4):
+                xs_t = xpool.tile([P, 2048], BF16, name="xs", bufs=4)
+                nc.sync.dma_start(out=xs_t[:], in_=x_v[:, br, :])
+                xs.append(xs_t)
+            load_k(1, [(0, NL)])
+            load_k(2, [(0, NL)])
+            load_bias(0)
+            load_k(3, [(0, NL)])
 
-        interleave(0)
+            interleave(0)
 
-        for br in range(4):
-            xh = xpool.tile([P, 2048], BF16, name="xh")
-            nc.vector.tensor_copy(
-                out=xh[:].rearrange("p (c r e) -> p c r e", c=4, r=16),
-                in_=xs[br][:].rearrange("p (r c e) -> p c r e", r=16, c=4),
-            )
-            words = xh[:].bitcast(F32)
-            hg = xpool.tile([P, 2048], BF16, name="hg", align_bytes=64)
-            hgw = hg[:].bitcast(F32)
-            for h2 in range(2):
-                xt = ps_x.tile([P, 512], F32, name="xt")
-                for jj in range(2):
-                    for u in range(2):
-                        w0 = (h2 * 2 + jj) * 256
-                        nc.tensor.transpose(
-                            xt[:, (jj * 2 + u) * P : (jj * 2 + u + 1) * P],
-                            words[:, w0 + u : w0 + 256 : 2],
-                            ident[:],
-                        )
-                nc.scalar.copy(
-                    out=hgw[:, h2 * 512 : (h2 + 1) * 512].rearrange(
-                        "p (j b u) -> p j b u", j=2, u=2
-                    ),
-                    in_=xt[:].rearrange("p (j u b) -> p j b u", j=2, u=2),
+            for br in range(4):
+                xh = xpool.tile([P, 2048], BF16, name="xh")
+                nc.vector.tensor_copy(
+                    out=xh[:].rearrange("p (c r e) -> p c r e", c=4, r=16),
+                    in_=xs[br][:].rearrange("p (r c e) -> p c r e", r=16, c=4),
                 )
-            nc.vector.quantize_mx(
-                out=hcodes[:, br * 512 : (br + 1) * 512].bitcast(FP8X4),
-                scales=hscales[:, br * 512 : (br + 1) * 512],
-                in_=hg[:],
-            )
+                if br == 0:
+                    quantize(0)
+                words = xh[:].bitcast(F32)
+                hg = xpool.tile([P, 2048], BF16, name="hg", align_bytes=64)
+                hgw = hg[:].bitcast(F32)
+                for h2 in range(2):
+                    xt = ps_x.tile([P, 512], F32, name="xt")
+                    for jj in range(2):
+                        for u in range(2):
+                            w0 = (h2 * 2 + jj) * 256
+                            nc.tensor.transpose(
+                                xt[:, (jj * 2 + u) * P : (jj * 2 + u + 1) * P],
+                                words[:, w0 + u : w0 + 256 : 2],
+                                ident[:],
+                            )
+                    nc.scalar.copy(
+                        out=hgw[:, h2 * 512 : (h2 + 1) * 512].rearrange(
+                            "p (j b u) -> p j b u", j=2, u=2
+                        ),
+                        in_=xt[:].rearrange("p (j u b) -> p j b u", j=2, u=2),
+                    )
+                nc.vector.quantize_mx(
+                    out=hcodes[:, br * 512 : (br + 1) * 512].bitcast(FP8X4),
+                    scales=hscales[:, br * 512 : (br + 1) * 512],
+                    in_=hg[:],
+                )
+
+        fpool = ctx.enter_context(tc.tile_pool(name="fpool", bufs=1))
 
         for j in range(NJ):
             if j + 1 < NJ:
                 interleave(j + 1)
-            quantize(j)
+            if j > 0:
+                quantize(j)
             if j + 4 < NJ:
-                load_k(j + 4)
+                load_k(j + 4, [(0, NL)])
             if j % 4 == 1 and j // 4 + 1 < 4:
                 load_bias(j // 4 + 1)
             if j >= 1:
@@ -186,7 +198,6 @@ def tile_switchnet_fstar_pa_kernel(tc, x, k1, b1, out_0, out_1):
             matmul(j)
         evacuate(NJ - 1)
 
-        yf = y[:].rearrange("p r c -> p (r c)")
         wst = NR * NJ * NM // NST
         for s in range(NST):
             nc.sync.dma_start(out=o0_v[:, s * wst : (s + 1) * wst], in_=yf[:, s * wst : (s + 1) * wst])
@@ -206,23 +217,24 @@ def tile_switchnet_fstar_pa_kernel(tc, x, k1, b1, out_0, out_1):
         nc.vector.reciprocal(out=rcp[:], in_=amax[:])
         nc.vector.tensor_scalar(out=fac[:], in0=rcp[:], scalar1=448.0, scalar2=None, op0=ALU.mult)
 
-        wc = NR * NJ * NM // NCAST
-        for q in range(NCAST):
-            f8 = const.tile([P, wc], FP8, name="f8_%d" % q)
+        for q in range(len(CASTS)):
+            a0, wc = CASTS[q]
+            vs = wc * VSHARE // 32
+            f8 = fpool.tile([P, wc], FP8, name="f8_%d" % q)
             nc.vector.tensor_scalar(
-                out=f8[:, 0:VS],
-                in0=yf[:, q * wc : q * wc + VS],
+                out=f8[:, 0:vs],
+                in0=yf[:, a0 : a0 + vs],
                 scalar1=fac[:, 0:1],
                 scalar2=None,
                 op0=ALU.mult,
                 saturate=False,
             )
             nc.scalar.activation(
-                out=f8[:, VS:wc],
-                in_=yf[:, q * wc + VS : (q + 1) * wc],
+                out=f8[:, vs:wc],
+                in_=yf[:, a0 + vs : a0 + wc],
                 func=ACT.Identity,
                 scale=fac[:, 0:1],
                 bias=zeros[:, 0:1],
                 saturate=False,
             )
-            nc.sync.dma_start(out=o1_v[:, q * wc : (q + 1) * wc], in_=f8[:].bitcast(U8))
+            nc.sync.dma_start(out=o1_v[:, a0 : a0 + wc], in_=f8[:].bitcast(U8))

@@ -23,7 +23,7 @@ NM = 8
 HALF = 512
 FLOPS = 2 * NB * NJ * NK * NL
 
-CV = 448
+CV = 384
 NRED = 8
 NST = 8
 CASTS = [(0, 4096), (4096, 4096), (8192, 4096), (12288, 2048), (14336, 2048)]
@@ -39,9 +39,9 @@ def tile_switchnet_fstar_pa_kernel(tc, x, k1, b1, out_0, out_1):
 
     with ExitStack() as ctx:
         const = ctx.enter_context(tc.tile_pool(name="const", bufs=1))
-        kpool = ctx.enter_context(tc.tile_pool(name="kpool", bufs=3))
+        kpool = ctx.enter_context(tc.tile_pool(name="kpool", bufs=4))
         ps_x = ctx.enter_context(tc.psum_pool(name="ps_x", bufs=2))
-        ps_a = ctx.enter_context(tc.psum_pool(name="ps_a", bufs=4))
+        ps_a = ctx.enter_context(tc.psum_pool(name="ps_a", bufs=5))
         ps_t = ctx.enter_context(tc.psum_pool(name="ps_t", bufs=1))
 
         zeros = const.tile([P, 1], F32, name="zeros")
@@ -74,7 +74,7 @@ def tile_switchnet_fstar_pa_kernel(tc, x, k1, b1, out_0, out_1):
             return HALF if j == NJ - 1 else CV
 
         def load_k(j, cuts):
-            raw = kpool.tile([P, 4, NL], BF16, name="raw", bufs=4)
+            raw = kpool.tile([P, 4, NL], BF16, name="raw", bufs=5)
             src = k1[j].rearrange("(p t) c -> p t c", t=4)
             for a, b in cuts:
                 nc.sync.dma_start(out=raw[:, :, a:b], in_=src[:, :, a:b])
@@ -146,6 +146,7 @@ def tile_switchnet_fstar_pa_kernel(tc, x, k1, b1, out_0, out_1):
             load_k(2, [(0, NL)])
             load_bias(0)
             load_k(3, [(0, NL)])
+            load_k(4, [(0, NL)])
 
             interleave(0)
 
@@ -189,8 +190,8 @@ def tile_switchnet_fstar_pa_kernel(tc, x, k1, b1, out_0, out_1):
                 interleave(j + 1)
             if j > 0:
                 quantize(j)
-            if j + 4 < NJ:
-                load_k(j + 4, [(0, NL)])
+            if j + 5 < NJ:
+                load_k(j + 5, [(0, NL)])
             if j % 4 == 1 and j // 4 + 1 < 4:
                 load_bias(j // 4 + 1)
             if j >= 1:

@@ -24,6 +24,7 @@ HALF = 512
 FLOPS = 2 * NB * NJ * NK * NL
 
 CV = 384
+RUN = 8
 NRED = 8
 NST = 8
 CASTS = [(0, 4096), (4096, 4096), (8192, 4096), (12288, 2048), (14336, 2048)]
@@ -87,8 +88,8 @@ def tile_switchnet_fstar_pa_kernel(tc, x, k1, b1, out_0, out_1):
 
         def lace(eng_copy, grp, raw, a, b):
             eng_copy(
-                out=grp[:, a:b, :].rearrange("p (c i) t -> p c t i", i=4),
-                in_=raw[:, :, a:b].rearrange("p t (c i) -> p c t i", i=4),
+                out=grp[:, a:b, :].rearrange("p (c i) t -> p c t i", i=RUN),
+                in_=raw[:, :, a:b].rearrange("p t (c i) -> p c t i", i=RUN),
             )
 
         def interleave(j):

@@ -24,6 +24,7 @@ HALF = 512
 FLOPS = 2 * NB * NJ * NK * NL
 
 CV = 384
+NRAW = 6
 RUN = 8
 NRED = 8
 NST = 8
@@ -75,7 +76,7 @@ def tile_switchnet_fstar_pa_kernel(tc, x, k1, b1, out_0, out_1):
             return HALF if j == NJ - 1 else CV
 
         def load_k(j, cuts):
-            raw = kpool.tile([P, 4, NL], BF16, name="raw", bufs=5)
+            raw = kpool.tile([P, 4, NL], BF16, name="raw", bufs=NRAW)
             src = k1[j].rearrange("(p t) c -> p t c", t=4)
             for a, b in cuts:
                 nc.sync.dma_start(out=raw[:, :, a:b], in_=src[:, :, a:b])
@@ -148,6 +149,7 @@ def tile_switchnet_fstar_pa_kernel(tc, x, k1, b1, out_0, out_1):
             load_bias(0)
             load_k(3, [(0, NL)])
             load_k(4, [(0, NL)])
+            load_k(5, [(0, NL)])
 
             interleave(0)
 
@@ -191,8 +193,8 @@ def tile_switchnet_fstar_pa_kernel(tc, x, k1, b1, out_0, out_1):
                 interleave(j + 1)
             if j > 0:
                 quantize(j)
-            if j + 5 < NJ:
-                load_k(j + 5, [(0, NL)])
+            if j + NRAW < NJ:
+                load_k(j + NRAW, [(0, NL)])
             if j % 4 == 1 and j // 4 + 1 < 4:
                 load_bias(j // 4 + 1)
             if j >= 1:

@@ -24,6 +24,11 @@ HALF = 512
 FLOPS = 2 * NB * NJ * NK * NL
 
 CV = 384
+GV = 288
+GG = 128
+GFIRST = 4
+GLAST = 14
+GAHEAD = 4
 NRAW = 6
 RUN = 8
 NRED = 8
@@ -93,11 +98,31 @@ def tile_switchnet_fstar_pa_kernel(tc, x, k1, b1, out_0, out_1):
                 in_=raw[:, :, a:b].rearrange("p t (c i) -> p c t i", i=RUN),
             )
 
-        def interleave(j):
+        def helped(j):
+            return GFIRST <= j <= GLAST
+
+        def glace(j):
             grp = kpool.tile([P, NL, 4], BF16, name="grp", align_bytes=64)
-            lace(nc.vector.tensor_copy, grp, raws[j], 0, split(j))
-            lace(nc.scalar.copy, grp, raws[j], split(j), NL)
+            nc.gpsimd.tensor_scalar(
+                out=grp[:, GV : GV + GG, :].rearrange("p (c i) t -> p c t i", i=RUN),
+                in0=raws[j][:, :, GV : GV + GG].rearrange("p t (c i) -> p c t i", i=RUN),
+                scalar1=1.0,
+                scalar2=0.0,
+                op0=ALU.mult,
+                op1=ALU.add,
+            )
             grps[j] = grp
+
+        def interleave(j):
+            if helped(j):
+                grp = grps[j]
+                lace(nc.vector.tensor_copy, grp, raws[j], 0, GV)
+                lace(nc.scalar.copy, grp, raws[j], GV + GG, NL)
+            else:
+                grp = kpool.tile([P, NL, 4], BF16, name="grp", align_bytes=64)
+                lace(nc.vector.tensor_copy, grp, raws[j], 0, split(j))
+                lace(nc.scalar.copy, grp, raws[j], split(j), NL)
+                grps[j] = grp
 
         def quantize(j):
             kc = kpool.tile([P, NL], U32, name="kc", align_bytes=64)
@@ -193,6 +218,8 @@ def tile_switchnet_fstar_pa_kernel(tc, x, k1, b1, out_0, out_1):
                 interleave(j + 1)
             if j > 0:
                 quantize(j)
+            if helped(j + GAHEAD):
+                glace(j + GAHEAD)
             if j + NRAW < NJ:
                 load_k(j + NRAW, [(0, NL)])
             if j % 4 == 1 and j // 4 + 1 < 4:

@@ -28,7 +28,6 @@ GV = 288
 GG = 128
 GFIRST = 4
 GLAST = 14
-GAHEAD = 4
 NRAW = 6
 RUN = 8
 NRED = 8
@@ -101,28 +100,26 @@ def tile_switchnet_fstar_pa_kernel(tc, x, k1, b1, out_0, out_1):
         def helped(j):
             return GFIRST <= j <= GLAST
 
-        def glace(j):
-            grp = kpool.tile([P, NL, 4], BF16, name="grp", align_bytes=64)
+        def glace(grp, j):
             nc.gpsimd.tensor_scalar(
-                out=grp[:, GV : GV + GG, :].rearrange("p (c i) t -> p c t i", i=RUN),
-                in0=raws[j][:, :, GV : GV + GG].rearrange("p t (c i) -> p c t i", i=RUN),
+                out=grp[:, GV : GV + GG, :],
+                in0=raws[j][:, :, GV : GV + GG].rearrange("p t c -> p c t"),
                 scalar1=1.0,
                 scalar2=0.0,
                 op0=ALU.mult,
                 op1=ALU.add,
             )
-            grps[j] = grp
 
         def interleave(j):
+            grp = kpool.tile([P, NL, 4], BF16, name="grp", align_bytes=64)
             if helped(j):
-                grp = grps[j]
+                glace(grp, j)
                 lace(nc.vector.tensor_copy, grp, raws[j], 0, GV)
                 lace(nc.scalar.copy, grp, raws[j], GV + GG, NL)
             else:
-                grp = kpool.tile([P, NL, 4], BF16, name="grp", align_bytes=64)
                 lace(nc.vector.tensor_copy, grp, raws[j], 0, split(j))
                 lace(nc.scalar.copy, grp, raws[j], split(j), NL)
-                grps[j] = grp
+            grps[j] = grp
 
         def quantize(j):
             kc = kpool.tile([P, NL], U32, name="kc", align_bytes=64)
@@ -218,8 +215,6 @@ def tile_switchnet_fstar_pa_kernel(tc, x, k1, b1, out_0, out_1):
                 interleave(j + 1)
             if j > 0:
                 quantize(j)
-            if helped(j + GAHEAD):
-                glace(j + GAHEAD)
             if j + NRAW < NJ:
                 load_k(j + NRAW, [(0, NL)])
             if j % 4 == 1 and j // 4 + 1 < 4:

@@ -24,8 +24,8 @@ HALF = 512
 FLOPS = 2 * NB * NJ * NK * NL
 
 CV = 384
-GV = 288
-GG = 128
+GV = 304
+GG = 96
 GFIRST = 4
 GLAST = 14
 NRAW = 6

@@ -30,7 +30,6 @@ GFIRST = 4
 GLAST = 14
 NRAW = 6
 RUN = 8
-NRED = 8
 NST = 8
 CASTS = [(0, 4096), (4096, 4096), (8192, 4096), (12288, 2048), (14336, 2048)]
 VSHARE = 21
@@ -56,7 +55,6 @@ def tile_switchnet_fstar_pa_kernel(tc, x, k1, b1, out_0, out_1):
         hcodes = const.tile([P, NJ * NB], U32, name="hcodes", align_bytes=64)
         hscales = const.tile([P, NJ * NB], U8, name="hscales", align_bytes=64)
         y = const.tile([P, NR, NJ * NM], F32, name="y")
-        stats = const.tile([P, NRED], F32, name="stats")
         pmax = const.tile([P, 1], F32, name="pmax")
         amax = const.tile([P, 1], F32, name="amax")
         rcp = const.tile([P, 1], F32, name="rcp")
@@ -178,8 +176,8 @@ def tile_switchnet_fstar_pa_kernel(tc, x, k1, b1, out_0, out_1):
             for br in range(4):
                 xh = xpool.tile([P, 2048], BF16, name="xh")
                 nc.vector.tensor_copy(
-                    out=xh[:].rearrange("p (c r e) -> p c r e", c=4, r=16),
-                    in_=xs[br][:].rearrange("p (r c e) -> p c r e", r=16, c=4),
+                    out=xh[:].bitcast(F32).rearrange("p (c u r e) -> p c u r e", c=4, u=2, r=16),
+                    in_=xs[br][:].bitcast(F32).rearrange("p (r c e u) -> p c u r e", r=16, c=4, u=2),
                 )
                 if br == 0:
                     quantize(0)
@@ -193,7 +191,7 @@ def tile_switchnet_fstar_pa_kernel(tc, x, k1, b1, out_0, out_1):
                             w0 = (h2 * 2 + jj) * 256
                             nc.tensor.transpose(
                                 xt[:, (jj * 2 + u) * P : (jj * 2 + u + 1) * P],
-                                words[:, w0 + u : w0 + 256 : 2],
+                                words[:, w0 + u * P : w0 + (u + 1) * P],
                                 ident[:],
                             )
                     nc.scalar.copy(
@@ -227,16 +225,9 @@ def tile_switchnet_fstar_pa_kernel(tc, x, k1, b1, out_0, out_1):
         wst = NR * NJ * NM // NST
         for s in range(NST):
             nc.sync.dma_start(out=o0_v[:, s * wst : (s + 1) * wst], in_=yf[:, s * wst : (s + 1) * wst])
-        wred = NR * NJ * NM // NRED
-        for s in range(NRED):
-            nc.vector.tensor_reduce(
-                out=stats[:, s : s + 1],
-                in_=yf[:, s * wred : (s + 1) * wred],
-                axis=AX.X,
-                op=ALU.max,
-                apply_absolute_value=True,
-            )
-        nc.vector.tensor_reduce(out=pmax[:], in_=stats[:], axis=AX.X, op=ALU.max)
+        nc.vector.tensor_reduce(
+            out=pmax[:], in_=yf[:, :], axis=AX.X, op=ALU.max, apply_absolute_value=True
+        )
         tp = ps_t.tile([P, P], F32, name="tp")
         nc.tensor.transpose(tp[:], pmax[:, 0:1].to_broadcast([P, P]), ident[:])
         nc.vector.tensor_reduce(out=amax[:], in_=tp[:], axis=AX.X, op=ALU.max)

@@ -27,7 +27,8 @@ CV = 384
 GV = 304
 GG = 96
 GFIRST = 4
-GLAST = 14
+GLATE = 9
+GV2 = 256
 NRAW = 6
 RUN = 8
 NST = 8
@@ -74,9 +75,6 @@ def tile_switchnet_fstar_pa_kernel(tc, x, k1, b1, out_0, out_1):
         codes = {}
         accs = {}
 
-        def split(j):
-            return HALF if j == NJ - 1 else CV
-
         def load_k(j, cuts):
             raw = kpool.tile([P, 4, NL], BF16, name="raw", bufs=NRAW)
             src = k1[j].rearrange("(p t) c -> p t c", t=4)
@@ -96,12 +94,18 @@ def tile_switchnet_fstar_pa_kernel(tc, x, k1, b1, out_0, out_1):
             )
 
         def helped(j):
-            return GFIRST <= j <= GLAST
+            return GFIRST <= j
+
+        def vshare(j):
+            if j == NJ - 1:
+                return HALF - GG
+            return GV if j < GLATE else GV2
 
         def glace(grp, j):
+            gv = vshare(j)
             nc.gpsimd.tensor_scalar(
-                out=grp[:, GV : GV + GG, :],
-                in0=raws[j][:, :, GV : GV + GG].rearrange("p t c -> p c t"),
+                out=grp[:, gv : gv + GG, :],
+                in0=raws[j][:, :, gv : gv + GG].rearrange("p t c -> p c t"),
                 scalar1=1.0,
                 scalar2=0.0,
                 op0=ALU.mult,
@@ -112,11 +116,11 @@ def tile_switchnet_fstar_pa_kernel(tc, x, k1, b1, out_0, out_1):
             grp = kpool.tile([P, NL, 4], BF16, name="grp", align_bytes=64)
             if helped(j):
                 glace(grp, j)
-                lace(nc.vector.tensor_copy, grp, raws[j], 0, GV)
-                lace(nc.scalar.copy, grp, raws[j], GV + GG, NL)
+                lace(nc.vector.tensor_copy, grp, raws[j], 0, vshare(j))
+                lace(nc.scalar.copy, grp, raws[j], vshare(j) + GG, NL)
             else:
-                lace(nc.vector.tensor_copy, grp, raws[j], 0, split(j))
-                lace(nc.scalar.copy, grp, raws[j], split(j), NL)
+                lace(nc.vector.tensor_copy, grp, raws[j], 0, CV)
+                lace(nc.scalar.copy, grp, raws[j], CV, NL)
             grps[j] = grp
 
         def quantize(j):

@@ -28,7 +28,7 @@ GV = 304
 GG = 96
 GFIRST = 4
 GLATE = 9
-GV2 = 256
+GV2 = 224
 NRAW = 6
 RUN = 8
 NST = 8

from contextlib import ExitStack

import concourse.mybir as mybir
from concourse.masks import make_identity

F32 = mybir.dt.float32
BF16 = mybir.dt.bfloat16
U32 = mybir.dt.uint32
U8 = mybir.dt.uint8
FP8X4 = mybir.dt.float8_e4m3fn_x4
FP8 = mybir.dt.float8_e4m3fn
ALU = mybir.AluOpType
ACT = mybir.ActivationFunctionType
AX = mybir.AxisListType

P = 128
NB = 128
NJ = 16
NK = 512
NL = 1024
NR = 128
NM = 8
HALF = 512
FLOPS = 2 * NB * NJ * NK * NL

CV = 384
GV = 304
GG = 96
GFIRST = 4
GLATE = 9
GV2 = 224
NRAW = 6
RUN = 8
NST = 8
CASTS = [(0, 4096), (4096, 4096), (8192, 4096), (12288, 2048), (14336, 2048)]
VSHARE = 21


def tile_switchnet_fstar_pa_kernel(tc, x, k1, b1, out_0, out_1):
    nc = tc.nc
    x_v = x.rearrange("b (q g) c -> b q (g c)", q=4)
    b_v = b1.rearrange("o j l -> (o j l)")
    o0_v = out_0.rearrange("b r c -> b (r c)")
    o1_v = out_1.rearrange("b r c -> b (r c)")

    with ExitStack() as ctx:
        const = ctx.enter_context(tc.tile_pool(name="const", bufs=1))
        kpool = ctx.enter_context(tc.tile_pool(name="kpool", bufs=4))
        ps_x = ctx.enter_context(tc.psum_pool(name="ps_x", bufs=2))
        ps_a = ctx.enter_context(tc.psum_pool(name="ps_a", bufs=5))
        ps_t = ctx.enter_context(tc.psum_pool(name="ps_t", bufs=1))

        zeros = const.tile([P, 1], F32, name="zeros")
        warm = const.tile([P, 1], F32, name="warm")
        ident = const.tile([P, P], F32, name="ident")
        hcodes = const.tile([P, NJ * NB], U32, name="hcodes", align_bytes=64)
        hscales = const.tile([P, NJ * NB], U8, name="hscales", align_bytes=64)
        y = const.tile([P, NR, NJ * NM], F32, name="y")
        pmax = const.tile([P, 1], F32, name="pmax")
        amax = const.tile([P, 1], F32, name="amax")
        rcp = const.tile([P, 1], F32, name="rcp")
        fac = const.tile([P, 1], F32, name="fac")
        bias = []
        for g in range(4):
            bias_g = const.tile([P, 4 * NL], BF16, name="bias%d" % g)
            bias.append(bias_g)
        yf = y[:].rearrange("p r c -> p (r c)")

        nc.vector.memset(zeros[:], 0.0)
        nc.scalar.activation(out=warm[:], in_=zeros[:], func=ACT.Identity)
        make_identity(nc, ident[:])

        raws = {}
        grps = {}
        codes = {}
        accs = {}

        def load_k(j, cuts):
            raw = kpool.tile([P, 4, NL], BF16, name="raw", bufs=NRAW)
            src = k1[j].rearrange("(p t) c -> p t c", t=4)
            for a, b in cuts:
                nc.sync.dma_start(out=raw[:, :, a:b], in_=src[:, :, a:b])
            raws[j] = raw

        def load_bias(g):
            nc.sync.dma_start(
                out=bias[g][:], in_=b_v[g * 4 * NL : (g + 1) * 4 * NL].partition_broadcast(P)
            )

        def lace(eng_copy, grp, raw, a, b):
            eng_copy(
                out=grp[:, a:b, :].rearrange("p (c i) t -> p c t i", i=RUN),
                in_=raw[:, :, a:b].rearrange("p t (c i) -> p c t i", i=RUN),
            )

        def helped(j):
            return GFIRST <= j

        def vshare(j):
            if j == NJ - 1:
                return HALF - GG
            return GV if j < GLATE else GV2

        def glace(grp, j):
            gv = vshare(j)
            nc.gpsimd.tensor_scalar(
                out=grp[:, gv : gv + GG, :],
                in0=raws[j][:, :, gv : gv + GG].rearrange("p t c -> p c t"),
                scalar1=1.0,
                scalar2=0.0,
                op0=ALU.mult,
                op1=ALU.add,
            )

        def interleave(j):
            grp = kpool.tile([P, NL, 4], BF16, name="grp", align_bytes=64)
            if helped(j):
                glace(grp, j)
                lace(nc.vector.tensor_copy, grp, raws[j], 0, vshare(j))
                lace(nc.scalar.copy, grp, raws[j], vshare(j) + GG, NL)
            else:
                lace(nc.vector.tensor_copy, grp, raws[j], 0, CV)
                lace(nc.scalar.copy, grp, raws[j], CV, NL)
            grps[j] = grp

        def quantize(j):
            kc = kpool.tile([P, NL], U32, name="kc", align_bytes=64)
            ks = kpool.tile([P, NL], U8, name="ks", align_bytes=64)
            cuts = [(0, HALF), (HALF, NL)] if j == NJ - 1 else [(0, NL)]
            for a, b in cuts:
                nc.vector.quantize_mx(
                    out=kc[:, a:b].bitcast(FP8X4),
                    scales=ks[:, a:b],
                    in_=grps[j][:, a:b, :].rearrange("p c t -> p (c t)"),
                )
            codes[j] = (kc, ks)

        def matmul(j):
            kc, ks = codes[j]
            for hf in range(2):
                acc = ps_a.tile([P, HALF], F32, name="acc")
                nc.tensor.matmul_mx(
                    out=acc[:],
                    lhsT=hcodes[:, j * NB : (j + 1) * NB].bitcast(FP8X4),
                    lhsT_scale=hscales[:, j * NB : (j + 1) * NB],
                    rhs=kc[:, hf * HALF : (hf + 1) * HALF].bitcast(FP8X4),
                    rhs_scale=ks[:, hf * HALF : (hf + 1) * HALF],
                    start=True,
                    stop=True,
                )
                accs[(j, hf)] = acc

        def evacuate(j):
            for hf in range(2):
                c0 = j * NM + hf * 4
                b0 = (j % 4) * NL + hf * HALF
                nc.vector.tensor_tensor(
                    out=y[:, :, c0 : c0 + 4],
                    in0=accs[(j, hf)][:].rearrange("p (m r) -> p r m", m=4),
                    in1=bias[j // 4][:, b0 : b0 + HALF].rearrange("p (m r) -> p r m", m=4),
                    op=ALU.add,
                )

        load_k(0, [(CV, NL), (0, CV)])
        with tc.tile_pool(name="xpool", bufs=2) as xpool:
            xs = []
            for br in range(4):
                xs_t = xpool.tile([P, 2048], BF16, name="xs", bufs=4)
                nc.sync.dma_start(out=xs_t[:], in_=x_v[:, br, :])
                xs.append(xs_t)
            load_k(1, [(0, NL)])
            load_k(2, [(0, NL)])
            load_bias(0)
            load_k(3, [(0, NL)])
            load_k(4, [(0, NL)])
            load_k(5, [(0, NL)])

            interleave(0)

            for br in range(4):
                xh = xpool.tile([P, 2048], BF16, name="xh")
                nc.vector.tensor_copy(
                    out=xh[:].bitcast(F32).rearrange("p (c u r e) -> p c u r e", c=4, u=2, r=16),
                    in_=xs[br][:].bitcast(F32).rearrange("p (r c e u) -> p c u r e", r=16, c=4, u=2),
                )
                if br == 0:
                    quantize(0)
                words = xh[:].bitcast(F32)
                hg = xpool.tile([P, 2048], BF16, name="hg", align_bytes=64)
                hgw = hg[:].bitcast(F32)
                for h2 in range(2):
                    xt = ps_x.tile([P, 512], F32, name="xt")
                    for jj in range(2):
                        for u in range(2):
                            w0 = (h2 * 2 + jj) * 256
                            nc.tensor.transpose(
                                xt[:, (jj * 2 + u) * P : (jj * 2 + u + 1) * P],
                                words[:, w0 + u * P : w0 + (u + 1) * P],
                                ident[:],
                            )
                    nc.scalar.copy(
                        out=hgw[:, h2 * 512 : (h2 + 1) * 512].rearrange(
                            "p (j b u) -> p j b u", j=2, u=2
                        ),
                        in_=xt[:].rearrange("p (j u b) -> p j b u", j=2, u=2),
                    )
                nc.vector.quantize_mx(
                    out=hcodes[:, br * 512 : (br + 1) * 512].bitcast(FP8X4),
                    scales=hscales[:, br * 512 : (br + 1) * 512],
                    in_=hg[:],
                )

        fpool = ctx.enter_context(tc.tile_pool(name="fpool", bufs=1))

        for j in range(NJ):
            if j + 1 < NJ:
                interleave(j + 1)
            if j > 0:
                quantize(j)
            if j + NRAW < NJ:
                load_k(j + NRAW, [(0, NL)])
            if j % 4 == 1 and j // 4 + 1 < 4:
                load_bias(j // 4 + 1)
            if j >= 1:
                evacuate(j - 1)
            matmul(j)
        evacuate(NJ - 1)

        wst = NR * NJ * NM // NST
        for s in range(NST):
            nc.sync.dma_start(out=o0_v[:, s * wst : (s + 1) * wst], in_=yf[:, s * wst : (s + 1) * wst])
        nc.vector.tensor_reduce(
            out=pmax[:], in_=yf[:, :], axis=AX.X, op=ALU.max, apply_absolute_value=True
        )
        tp = ps_t.tile([P, P], F32, name="tp")
        nc.tensor.transpose(tp[:], pmax[:, 0:1].to_broadcast([P, P]), ident[:])
        nc.vector.tensor_reduce(out=amax[:], in_=tp[:], axis=AX.X, op=ALU.max)
        nc.vector.reciprocal(out=rcp[:], in_=amax[:])
        nc.vector.tensor_scalar(out=fac[:], in0=rcp[:], scalar1=448.0, scalar2=None, op0=ALU.mult)

        for q in range(len(CASTS)):
            a0, wc = CASTS[q]
            vs = wc * VSHARE // 32
            f8 = fpool.tile([P, wc], FP8, name="f8_%d" % q)
            nc.vector.tensor_scalar(
                out=f8[:, 0:vs],
                in0=yf[:, a0 : a0 + vs],
                scalar1=fac[:, 0:1],
                scalar2=None,
                op0=ALU.mult,
                saturate=False,
            )
            nc.scalar.activation(
                out=f8[:, vs:wc],
                in_=yf[:, a0 + vs : a0 + wc],
                func=ACT.Identity,
                scale=fac[:, 0:1],
                bias=zeros[:, 0:1],
                saturate=False,
            )
            nc.sync.dma_start(out=o1_v[:, a0 : a0 + wc], in_=f8[:].bitcast(U8))
